import numpy as np
import ml_dtypes


def mxq(x, axis, fmt="e4m3"):
    dtype, down = {"e4m3": (ml_dtypes.float8_e4m3fn, 7), "e5m2": (ml_dtypes.float8_e5m2, 14)}[fmt]
    v = np.moveaxis(np.asarray(x, np.float32).astype(ml_dtypes.bfloat16).astype(np.float64), axis, -1)
    blocks = v.reshape(v.shape[:-1] + (-1, 32))
    amax = np.abs(blocks).max(-1, keepdims=True)
    byte = np.maximum(np.where(amax > 0, np.frexp(amax)[1] - 1 + 127, 0) - down, 1)
    scale = np.exp2(byte - 127.0)
    codes = (blocks / scale).astype(np.float32).astype(dtype).astype(np.float64)
    return np.moveaxis((codes * scale).reshape(v.shape), -1, axis)


WIDE = False


def mx_kscale(k):
    if not WIDE:
        return np.ones(k)
    levels = np.array([20, -20, 10, -10, 0])
    a = np.random.permutation(np.resize(levels, k // 512 * 4)).reshape(k // 512, 4)
    idx = np.arange(k)
    return np.exp2(a[idx // 512, idx % 128 // 32])


BF16 = ml_dtypes.bfloat16


def bf(x):
    return np.asarray(x, np.float32).astype(BF16)


def f64(x):
    return np.asarray(x).astype(np.float64)


B, Nb1, Nw1, Nb2x, Nb2y, Nw2x, Nw2y, R, C = 128, 2, 16, 4, 2, 16, 16, 64, 2
J1 = Nb1 * Nb1
K1 = C * Nw1 * Nw1
J3 = Nb2x * Nb2y
L1 = J3 * R
J2 = J3 * J1


def setup_inputs():
    u = mx_kscale(L1)
    x = np.random.standard_normal((B, Nb1 * Nw1 * Nb1 * Nw1, C))
    k1 = np.random.standard_normal((J1, K1, L1)) / np.sqrt(K1) / u[None, None, :]
    b1 = np.random.standard_normal((1, J1, L1)) * 0.3
    gy = np.random.standard_normal((B, J1, J3, R)) * np.exp2(np.random.randint(-12, 1, (B, J1, 1, 1))) * 4.0
    gy = gy * u.reshape(J3, R)[None, None, :, :]
    g = gy.transpose(0, 3, 1, 2).reshape(B, J2, R)
    return {"x": bf(x), "k1": bf(k1), "b1": bf(b1), "grad_out": bf(g)}


def reference(x, k1, b1, grad_out):
    gy = f64(grad_out).reshape(B, R, J1, J3).transpose(2, 0, 3, 1).reshape(J1, B, L1)
    gh = mxq(gy, 2, "e5m2") @ mxq(f64(k1), 2, "e4m3").transpose(0, 2, 1)
    gh = gh.transpose(1, 0, 2).reshape(B, Nb1, Nb1, Nw1, Nw1, C).transpose(0, 1, 3, 2, 4, 5)
    return gh.reshape(B, Nb1 * Nw1 * Nb1 * Nw1, C)

@@ -1,0 +1,147 @@
+from contextlib import ExitStack
+
+import concourse.mybir as mybir
+from concourse.masks import make_identity
+
+BF16 = mybir.dt.bfloat16
+F32 = mybir.dt.float32
+U32 = mybir.dt.uint32
+U8 = mybir.dt.uint8
+E4M3_X4 = mybir.dt.float8_e4m3fn_x4
+E5M2_X4 = mybir.dt.float8_e5m2_x4
+
+P = 128
+SAMPLES = 128
+BLOCKS = 4
+WINDOW = 512
+FEATURES = 512
+M_GROUPS = 8
+R_COEFFS = 64
+WORDS = FEATURES // 2
+CHUNK_ROWS = 256
+CHUNKS = BLOCKS * WINDOW // CHUNK_ROWS
+BANK = 512
+GRID_ROW = 64
+BLOCK_ROW = 32
+
+FLOPS = 2 * SAMPLES * BLOCKS * WINDOW * FEATURES
+BYTES = 2 * BLOCKS * WINDOW * FEATURES + 2 * SAMPLES * BLOCKS * FEATURES + 4 * SAMPLES * BLOCKS * WINDOW
+
+
+def tile_switchnet_fstar_pa_s_kernel(tc, x, k1, b1, grad_out, out):
+    nc = tc.nc
+    with ExitStack() as stack:
+        keep = stack.enter_context(tc.tile_pool(name="keep", bufs=1))
+        flipped = stack.enter_context(tc.psum_pool(name="flipped", bufs=4))
+        products = stack.enter_context(tc.psum_pool(name="products", bufs=4))
+
+        ident = keep.tile([P, P], F32)
+        make_identity(nc, ident[:])
+
+        g_sb = keep.tile([P, BLOCKS * FEATURES], BF16)
+        nc.sync.dma_start(out=g_sb[:], in_=grad_out.rearrange("b a r -> b (a r)"))
+        k_sb = []
+        for c in range(CHUNKS):
+            j, h = divmod(c, 2)
+            rows = keep.tile([P, 2 * FEATURES], BF16, name="k_sb%d" % c)
+            nc.sync.dma_start(
+                out=rows[:],
+                in_=k1[j, h * CHUNK_ROWS : (h + 1) * CHUNK_ROWS, :].rearrange("(q c) l -> q (c l)", c=2),
+            )
+            k_sb.append(rows)
+
+        gy_sb = keep.tile([P, BLOCKS * FEATURES], BF16)
+        switched = g_sb[:].rearrange("b (r j m) -> b j m r", r=R_COEFFS, j=BLOCKS, m=M_GROUPS)
+        unswitched = gy_sb[:].rearrange("b (j m r) -> b j m r", j=BLOCKS, m=M_GROUPS, r=R_COEFFS)
+        for j in range(BLOCKS):
+            if j < BLOCKS - 1:
+                nc.vector.tensor_copy(out=unswitched[:, j], in_=switched[:, j])
+            else:
+                nc.scalar.copy(out=unswitched[:, j], in_=switched[:, j])
+
+        gy_words = gy_sb[:].bitcast(F32)
+        gy_grouped = keep.tile([P, BLOCKS * SAMPLES * 4], BF16, align_bytes=64)
+        gy_grouped_words = gy_grouped[:].bitcast(F32)
+        gy_codes = keep.tile([P, BLOCKS * SAMPLES], U32, align_bytes=64)
+        gy_scales = keep.tile([P, BLOCKS * SAMPLES], U8, align_bytes=64)
+
+        def flip_gradient(pair):
+            bank = flipped.tile([P, BANK], F32, tag="bank")
+            for s in range(4):
+                col = pair * BANK + s * P
+                nc.tensor.transpose(bank[:, s * P : (s + 1) * P], gy_words[:, col : col + P], ident[:])
+            nc.vector.tensor_copy(
+                out=gy_grouped_words[:, pair * BANK : (pair + 1) * BANK].rearrange(
+                    "p (j b u) -> p j b u", j=2, b=SAMPLES, u=2
+                ),
+                in_=bank[:].rearrange("p (j u b) -> p j b u", j=2, u=2, b=SAMPLES),
+            )
+
+        k_grouped = []
+        k_codes = []
+        k_scales = []
+        for j in range(BLOCKS):
+            k_codes.append(keep.tile([P, WINDOW], U32, name="k_codes%d" % j, align_bytes=64))
+            k_scales.append(keep.tile([P, WINDOW], U8, name="k_scales%d" % j, align_bytes=64))
+        for c in range(CHUNKS):
+            k_grouped.append(keep.tile([P, CHUNK_ROWS * 4], BF16, name="k_grouped%d" % c, align_bytes=64))
+
+        def flip_chunk(c):
+            words = k_sb[c][:].bitcast(F32)
+            bank = flipped.tile([P, BANK], F32, tag="bank")
+            for s in range(4):
+                nc.tensor.transpose(bank[:, s * P : (s + 1) * P], words[:, s * P : (s + 1) * P], ident[:])
+            nc.scalar.copy(
+                out=k_grouped[c][:].bitcast(F32).rearrange("p (q s) -> p q s", s=4),
+                in_=bank[:].rearrange("p (s q) -> p q s", s=4),
+            )
+
+        def quantise_chunk(c):
+            j, h = divmod(c, 2)
+            cols = slice(h * CHUNK_ROWS, (h + 1) * CHUNK_ROWS)
+            nc.vector.quantize_mx(
+                out=k_codes[j][:, cols].bitcast(E4M3_X4),
+                scales=k_scales[j][:, cols],
+                in_=k_grouped[c][:],
+            )
+
+        out_sb = []
+        for block_row in range(2):
+            out_sb.append(keep.tile([P, 2 * WINDOW], F32, name="out_sb%d" % block_row))
+        out_flat = out.rearrange("b g c -> b (g c)")
+
+        def multiply_block(j):
+            block_row, block_col = divmod(j, 2)
+            samples = slice(j * SAMPLES, (j + 1) * SAMPLES)
+            acc = products.tile([P, WINDOW], F32, tag="acc")
+            nc.tensor.matmul_mx(
+                out=acc[:],
+                lhsT=gy_codes[:, samples].bitcast(E5M2_X4),
+                lhsT_scale=gy_scales[:, samples],
+                rhs=k_codes[j][:].bitcast(E4M3_X4),
+                rhs_scale=k_scales[j][:],
+                start=True,
+                stop=True,
+            )
+            on_grid = out_sb[block_row][:].rearrange("b (w c x) -> b c w x", c=2, x=BLOCK_ROW)[:, block_col]
+            window = acc[:].rearrange("b (w x) -> b w x", x=BLOCK_ROW)
+            if block_col == 0:
+                nc.scalar.copy(out=on_grid, in_=window)
+            else:
+                nc.vector.tensor_copy(out=on_grid, in_=window)
+                nc.sync.dma_start(
+                    out=out_flat[:, block_row * 2 * WINDOW : (block_row + 1) * 2 * WINDOW],
+                    in_=out_sb[block_row][:],
+                )
+
+        flip_chunk(0)
+        flip_gradient(0)
+        flip_gradient(1)
+        nc.vector.quantize_mx(out=gy_codes[:].bitcast(E5M2_X4), scales=gy_scales[:], in_=gy_grouped[:])
+        for step in range(1, CHUNKS + 2):
+            if step < CHUNKS:
+                flip_chunk(step)
+            if step - 1 < CHUNKS:
+                quantise_chunk(step - 1)
+            if step >= 3 and step % 2 == 1:
+                multiply_block((step - 3) // 2)

@@ -32,8 +32,8 @@ def tile_switchnet_fstar_pa_s_kernel(tc, x, k1, b1, grad_out, out):
     nc = tc.nc
     with ExitStack() as stack:
         keep = stack.enter_context(tc.tile_pool(name="keep", bufs=1))
-        flipped = stack.enter_context(tc.psum_pool(name="flipped", bufs=4))
-        products = stack.enter_context(tc.psum_pool(name="products", bufs=4))
+        psum = stack.enter_context(tc.psum_pool(name="psum", bufs=8))
+        stack.enter_context(tc.manual_schedule())
 
         ident = keep.tile([P, P], F32)
         make_identity(nc, ident[:])
@@ -65,12 +65,12 @@ def tile_switchnet_fstar_pa_s_kernel(tc, x, k1, b1, grad_out, out):
         gy_codes = keep.tile([P, BLOCKS * SAMPLES], U32, align_bytes=64)
         gy_scales = keep.tile([P, BLOCKS * SAMPLES], U8, align_bytes=64)
 
-        def flip_gradient(pair):
-            bank = flipped.tile([P, BANK], F32, tag="bank")
+        def flip_gradient(pair, copy_out):
+            bank = psum.tile([P, BANK], F32, tag="bank")
             for s in range(4):
                 col = pair * BANK + s * P
                 nc.tensor.transpose(bank[:, s * P : (s + 1) * P], gy_words[:, col : col + P], ident[:])
-            nc.vector.tensor_copy(
+            copy_out(
                 out=gy_grouped_words[:, pair * BANK : (pair + 1) * BANK].rearrange(
                     "p (j b u) -> p j b u", j=2, b=SAMPLES, u=2
                 ),
@@ -88,7 +88,7 @@ def tile_switchnet_fstar_pa_s_kernel(tc, x, k1, b1, grad_out, out):
 
         def flip_chunk(c):
             words = k_sb[c][:].bitcast(F32)
-            bank = flipped.tile([P, BANK], F32, tag="bank")
+            bank = psum.tile([P, BANK], F32, tag="bank")
             for s in range(4):
                 nc.tensor.transpose(bank[:, s * P : (s + 1) * P], words[:, s * P : (s + 1) * P], ident[:])
             nc.scalar.copy(
@@ -113,7 +113,7 @@ def tile_switchnet_fstar_pa_s_kernel(tc, x, k1, b1, grad_out, out):
         def multiply_block(j):
             block_row, block_col = divmod(j, 2)
             samples = slice(j * SAMPLES, (j + 1) * SAMPLES)
-            acc = products.tile([P, WINDOW], F32, tag="acc")
+            acc = psum.tile([P, WINDOW], F32, tag="bank")
             nc.tensor.matmul_mx(
                 out=acc[:],
                 lhsT=gy_codes[:, samples].bitcast(E5M2_X4),
@@ -125,23 +125,23 @@ def tile_switchnet_fstar_pa_s_kernel(tc, x, k1, b1, grad_out, out):
             )
             on_grid = out_sb[block_row][:].rearrange("b (w c x) -> b c w x", c=2, x=BLOCK_ROW)[:, block_col]
             window = acc[:].rearrange("b (w x) -> b w x", x=BLOCK_ROW)
-            if block_col == 0:
+            if block_row == 0:
                 nc.scalar.copy(out=on_grid, in_=window)
             else:
                 nc.vector.tensor_copy(out=on_grid, in_=window)
+            if block_col == 1:
                 nc.sync.dma_start(
                     out=out_flat[:, block_row * 2 * WINDOW : (block_row + 1) * 2 * WINDOW],
                     in_=out_sb[block_row][:],
                 )
 
         flip_chunk(0)
-        flip_gradient(0)
-        flip_gradient(1)
+        flip_gradient(0, nc.vector.tensor_copy)
+        flip_gradient(1, nc.scalar.copy)
+        quantise_chunk(0)
         nc.vector.quantize_mx(out=gy_codes[:].bitcast(E5M2_X4), scales=gy_scales[:], in_=gy_grouped[:])
-        for step in range(1, CHUNKS + 2):
-            if step < CHUNKS:
-                flip_chunk(step)
-            if step - 1 < CHUNKS:
-                quantise_chunk(step - 1)
-            if step >= 3 and step % 2 == 1:
-                multiply_block((step - 3) // 2)
+        for c in range(1, CHUNKS):
+            flip_chunk(c)
+            quantise_chunk(c)
+        for j in range(BLOCKS):
+            multiply_block(j)

@@ -23,6 +23,7 @@ CHUNKS = BLOCKS * WINDOW // CHUNK_ROWS
 BANK = 512
 GRID_ROW = 64
 BLOCK_ROW = 32
+WARM_MATMULS = 6
 
 FLOPS = 2 * SAMPLES * BLOCKS * WINDOW * FEATURES
 BYTES = 2 * BLOCKS * WINDOW * FEATURES + 2 * SAMPLES * BLOCKS * FEATURES + 4 * SAMPLES * BLOCKS * WINDOW
@@ -37,6 +38,10 @@ def tile_switchnet_fstar_pa_s_kernel(tc, x, k1, b1, grad_out, out):
 
         ident = keep.tile([P, P], F32)
         make_identity(nc, ident[:])
+
+        unread = psum.tile([P, BANK], F32, tag="bank")
+        for w in range(WARM_MATMULS):
+            nc.tensor.matmul(out=unread[:, :P], lhsT=ident[:], rhs=ident[:], start=True, stop=True)
 
         g_sb = keep.tile([P, BLOCKS * FEATURES], BF16)
         nc.sync.dma_start(out=g_sb[:], in_=grad_out.rearrange("b a r -> b (a r)"))

@@ -17,16 +17,24 @@ WINDOW = 512
 FEATURES = 512
 M_GROUPS = 8
 R_COEFFS = 64
-WORDS = FEATURES // 2
-CHUNK_ROWS = 256
-CHUNKS = BLOCKS * WINDOW // CHUNK_ROWS
 BANK = 512
-GRID_ROW = 64
 BLOCK_ROW = 32
+HALF = WINDOW // 2
 WARM_MATMULS = 6
 
 FLOPS = 2 * SAMPLES * BLOCKS * WINDOW * FEATURES
 BYTES = 2 * BLOCKS * WINDOW * FEATURES + 2 * SAMPLES * BLOCKS * FEATURES + 4 * SAMPLES * BLOCKS * WINDOW
+
+
+def pieces_of_k1():
+    pieces = []
+    for j in range(BLOCKS):
+        pieces.append((j, 0, HALF))
+        pieces.append((j, HALF, HALF))
+    j, first, rows = pieces.pop()
+    pieces.append((j, first, rows // 2))
+    pieces.append((j, first + rows // 2, rows // 2))
+    return pieces
 
 
 def tile_switchnet_fstar_pa_s_kernel(tc, x, k1, b1, grad_out, out):
@@ -45,15 +53,15 @@ def tile_switchnet_fstar_pa_s_kernel(tc, x, k1, b1, grad_out, out):
 
         g_sb = keep.tile([P, BLOCKS * FEATURES], BF16)
         nc.sync.dma_start(out=g_sb[:], in_=grad_out.rearrange("b a r -> b (a r)"))
+        pieces = pieces_of_k1()
         k_sb = []
-        for c in range(CHUNKS):
-            j, h = divmod(c, 2)
-            rows = keep.tile([P, 2 * FEATURES], BF16, name="k_sb%d" % c)
+        for n, (j, first, rows) in enumerate(pieces):
+            loaded = keep.tile([P, rows // P * FEATURES], BF16, name="k_sb%d" % n)
             nc.sync.dma_start(
-                out=rows[:],
-                in_=k1[j, h * CHUNK_ROWS : (h + 1) * CHUNK_ROWS, :].rearrange("(q c) l -> q (c l)", c=2),
+                out=loaded[:],
+                in_=k1[j, first : first + rows, :].rearrange("(q c) l -> q (c l)", c=rows // P),
             )
-            k_sb.append(rows)
+            k_sb.append(loaded)
 
         gy_sb = keep.tile([P, BLOCKS * FEATURES], BF16)
         switched = g_sb[:].rearrange("b (r j m) -> b j m r", r=R_COEFFS, j=BLOCKS, m=M_GROUPS)
@@ -70,44 +78,40 @@ def tile_switchnet_fstar_pa_s_kernel(tc, x, k1, b1, grad_out, out):
         gy_codes = keep.tile([P, BLOCKS * SAMPLES], U32, align_bytes=64)
         gy_scales = keep.tile([P, BLOCKS * SAMPLES], U8, align_bytes=64)
 
-        def flip_gradient(pair, copy_out):
+        def flip_gradient(pair):
             bank = psum.tile([P, BANK], F32, tag="bank")
             for s in range(4):
                 col = pair * BANK + s * P
                 nc.tensor.transpose(bank[:, s * P : (s + 1) * P], gy_words[:, col : col + P], ident[:])
-            copy_out(
+            nc.vector.tensor_copy(
                 out=gy_grouped_words[:, pair * BANK : (pair + 1) * BANK].rearrange(
                     "p (j b u) -> p j b u", j=2, b=SAMPLES, u=2
                 ),
                 in_=bank[:].rearrange("p (j u b) -> p j b u", j=2, u=2, b=SAMPLES),
             )
 
-        k_grouped = []
         k_codes = []
         k_scales = []
         for j in range(BLOCKS):
             k_codes.append(keep.tile([P, WINDOW], U32, name="k_codes%d" % j, align_bytes=64))
             k_scales.append(keep.tile([P, WINDOW], U8, name="k_scales%d" % j, align_bytes=64))
-        for c in range(CHUNKS):
-            k_grouped.append(keep.tile([P, CHUNK_ROWS * 4], BF16, name="k_grouped%d" % c, align_bytes=64))
 
-        def flip_chunk(c):
-            words = k_sb[c][:].bitcast(F32)
+        def flip_and_quantise_piece(n):
+            j, first, rows = pieces[n]
+            planes = 2 * rows // P
+            words = k_sb[n][:].bitcast(F32)
             bank = psum.tile([P, BANK], F32, tag="bank")
-            for s in range(4):
+            for s in range(planes):
                 nc.tensor.transpose(bank[:, s * P : (s + 1) * P], words[:, s * P : (s + 1) * P], ident[:])
+            grouped = keep.tile([P, rows * 4], BF16, name="k_grouped%d" % n, align_bytes=64)
             nc.scalar.copy(
-                out=k_grouped[c][:].bitcast(F32).rearrange("p (q s) -> p q s", s=4),
-                in_=bank[:].rearrange("p (s q) -> p q s", s=4),
+                out=grouped[:].bitcast(F32).rearrange("p (q s) -> p q s", s=planes),
+                in_=bank[:, : planes * P].rearrange("p (s q) -> p q s", s=planes),
             )
-
-        def quantise_chunk(c):
-            j, h = divmod(c, 2)
-            cols = slice(h * CHUNK_ROWS, (h + 1) * CHUNK_ROWS)
             nc.vector.quantize_mx(
-                out=k_codes[j][:, cols].bitcast(E4M3_X4),
-                scales=k_scales[j][:, cols],
-                in_=k_grouped[c][:],
+                out=k_codes[j][:, first : first + rows].bitcast(E4M3_X4),
+                scales=k_scales[j][:, first : first + rows],
+                in_=grouped[:],
             )
 
         out_sb = []
@@ -128,25 +132,25 @@ def tile_switchnet_fstar_pa_s_kernel(tc, x, k1, b1, grad_out, out):
                 start=True,
                 stop=True,
             )
-            on_grid = out_sb[block_row][:].rearrange("b (w c x) -> b c w x", c=2, x=BLOCK_ROW)[:, block_col]
-            window = acc[:].rearrange("b (w x) -> b w x", x=BLOCK_ROW)
-            if block_row == 0:
-                nc.scalar.copy(out=on_grid, in_=window)
-            else:
-                nc.vector.tensor_copy(out=on_grid, in_=window)
-            if block_col == 1:
-                nc.sync.dma_start(
-                    out=out_flat[:, block_row * 2 * WINDOW : (block_row + 1) * 2 * WINDOW],
-                    in_=out_sb[block_row][:],
-                )
+            on_grid = out_sb[block_row][:].rearrange("b (h w c x) -> b h c w x", h=2, c=2, x=BLOCK_ROW)
+            window = acc[:].rearrange("b (h w x) -> b h w x", h=2, x=BLOCK_ROW)
+            for half in range(2):
+                if block_row == 0:
+                    nc.scalar.copy(out=on_grid[:, half, block_col], in_=window[:, half])
+                else:
+                    nc.vector.tensor_copy(out=on_grid[:, half, block_col], in_=window[:, half])
+                if block_col == 1:
+                    first = (2 * block_row + half) * WINDOW
+                    nc.sync.dma_start(
+                        out=out_flat[:, first : first + WINDOW],
+                        in_=out_sb[block_row][:, half * WINDOW : (half + 1) * WINDOW],
+                    )
 
-        flip_chunk(0)
-        flip_gradient(0, nc.vector.tensor_copy)
-        flip_gradient(1, nc.scalar.copy)
-        quantise_chunk(0)
+        flip_and_quantise_piece(0)
+        flip_gradient(0)
+        flip_gradient(1)
         nc.vector.quantize_mx(out=gy_codes[:].bitcast(E5M2_X4), scales=gy_scales[:], in_=gy_grouped[:])
-        for c in range(1, CHUNKS):
-            flip_chunk(c)
-            quantise_chunk(c)
+        for n in range(1, len(pieces)):
+            flip_and_quantise_piece(n)
         for j in range(BLOCKS):
             multiply_block(j)

@@ -96,22 +96,28 @@ def tile_switchnet_fstar_pa_s_kernel(tc, x, k1, b1, grad_out, out):
             k_codes.append(keep.tile([P, WINDOW], U32, name="k_codes%d" % j, align_bytes=64))
             k_scales.append(keep.tile([P, WINDOW], U8, name="k_scales%d" % j, align_bytes=64))
 
-        def flip_and_quantise_piece(n):
+        k_grouped = []
+        for n, (j, first, rows) in enumerate(pieces):
+            k_grouped.append(keep.tile([P, rows * 4], BF16, name="k_grouped%d" % n, align_bytes=64))
+
+        def flip_piece(n):
             j, first, rows = pieces[n]
             planes = 2 * rows // P
             words = k_sb[n][:].bitcast(F32)
             bank = psum.tile([P, BANK], F32, tag="bank")
             for s in range(planes):
                 nc.tensor.transpose(bank[:, s * P : (s + 1) * P], words[:, s * P : (s + 1) * P], ident[:])
-            grouped = keep.tile([P, rows * 4], BF16, name="k_grouped%d" % n, align_bytes=64)
             nc.scalar.copy(
-                out=grouped[:].bitcast(F32).rearrange("p (q s) -> p q s", s=planes),
+                out=k_grouped[n][:].bitcast(F32).rearrange("p (q s) -> p q s", s=planes),
                 in_=bank[:, : planes * P].rearrange("p (s q) -> p q s", s=planes),
             )
+
+        def quantise_piece(n):
+            j, first, rows = pieces[n]
             nc.vector.quantize_mx(
                 out=k_codes[j][:, first : first + rows].bitcast(E4M3_X4),
                 scales=k_scales[j][:, first : first + rows],
-                in_=grouped[:],
+                in_=k_grouped[n][:],
             )
 
         out_sb = []
@@ -135,7 +141,7 @@ def tile_switchnet_fstar_pa_s_kernel(tc, x, k1, b1, grad_out, out):
             on_grid = out_sb[block_row][:].rearrange("b (h w c x) -> b h c w x", h=2, c=2, x=BLOCK_ROW)
             window = acc[:].rearrange("b (h w x) -> b h w x", h=2, x=BLOCK_ROW)
             for half in range(2):
-                if block_row == 0:
+                if block_col == 0:
                     nc.scalar.copy(out=on_grid[:, half, block_col], in_=window[:, half])
                 else:
                     nc.vector.tensor_copy(out=on_grid[:, half, block_col], in_=window[:, half])
@@ -146,11 +152,15 @@ def tile_switchnet_fstar_pa_s_kernel(tc, x, k1, b1, grad_out, out):
                         in_=out_sb[block_row][:, half * WINDOW : (half + 1) * WINDOW],
                     )
 
-        flip_and_quantise_piece(0)
+        flip_piece(0)
         flip_gradient(0)
+        flip_piece(1)
         flip_gradient(1)
         nc.vector.quantize_mx(out=gy_codes[:].bitcast(E5M2_X4), scales=gy_scales[:], in_=gy_grouped[:])
-        for n in range(1, len(pieces)):
-            flip_and_quantise_piece(n)
+        quantise_piece(0)
+        quantise_piece(1)
+        for n in range(2, len(pieces)):
+            flip_piece(n)
+            quantise_piece(n)
         for j in range(BLOCKS):
             multiply_block(j)

@@ -17,24 +17,14 @@ WINDOW = 512
 FEATURES = 512
 M_GROUPS = 8
 R_COEFFS = 64
+R_HALF = R_COEFFS // 2
 BANK = 512
 BLOCK_ROW = 32
-HALF = WINDOW // 2
-WARM_MATMULS = 6
+ROWS = 256
+WARM_MATMULS = 4
 
 FLOPS = 2 * SAMPLES * BLOCKS * WINDOW * FEATURES
 BYTES = 2 * BLOCKS * WINDOW * FEATURES + 2 * SAMPLES * BLOCKS * FEATURES + 4 * SAMPLES * BLOCKS * WINDOW
-
-
-def pieces_of_k1():
-    pieces = []
-    for j in range(BLOCKS):
-        pieces.append((j, 0, HALF))
-        pieces.append((j, HALF, HALF))
-    j, first, rows = pieces.pop()
-    pieces.append((j, first, rows // 2))
-    pieces.append((j, first + rows // 2, rows // 2))
-    return pieces
 
 
 def tile_switchnet_fstar_pa_s_kernel(tc, x, k1, b1, grad_out, out):
@@ -51,26 +41,49 @@ def tile_switchnet_fstar_pa_s_kernel(tc, x, k1, b1, grad_out, out):
         for w in range(WARM_MATMULS):
             nc.tensor.matmul(out=unread[:, :P], lhsT=ident[:], rhs=ident[:], start=True, stop=True)
 
-        g_sb = keep.tile([P, BLOCKS * FEATURES], BF16)
-        nc.sync.dma_start(out=g_sb[:], in_=grad_out.rearrange("b a r -> b (a r)"))
-        pieces = pieces_of_k1()
-        k_sb = []
-        for n, (j, first, rows) in enumerate(pieces):
-            loaded = keep.tile([P, rows // P * FEATURES], BF16, name="k_sb%d" % n)
+        g_flat = grad_out.rearrange("b a r -> b (a r)")
+        half_columns = R_HALF * BLOCKS * M_GROUPS
+        g_sb = {}
+        k_sb = {}
+
+        def load_gradient(half):
+            g_sb[half] = keep.tile([P, half_columns], BF16, name="g_sb%d" % half)
+            nc.sync.dma_start(out=g_sb[half][:], in_=g_flat[:, half * half_columns : (half + 1) * half_columns])
+
+        def load_piece(n):
+            j, half = divmod(n, 2)
+            k_sb[n] = keep.tile([P, 2 * FEATURES], BF16, name="k_sb%d" % n)
             nc.sync.dma_start(
-                out=loaded[:],
-                in_=k1[j, first : first + rows, :].rearrange("(q c) l -> q (c l)", c=rows // P),
+                out=k_sb[n][:],
+                in_=k1[j, half * ROWS : (half + 1) * ROWS, :].rearrange("(q c) l -> q (c l)", c=2),
             )
-            k_sb.append(loaded)
+
+        load_gradient(0)
+        load_gradient(1)
+        load_piece(0)
+        load_piece(1)
+        load_piece(2)
+        load_piece(3)
+        load_piece(4)
+        load_piece(5)
+        load_piece(6)
+        load_piece(7)
 
         gy_sb = keep.tile([P, BLOCKS * FEATURES], BF16)
-        switched = g_sb[:].rearrange("b (r j m) -> b j m r", r=R_COEFFS, j=BLOCKS, m=M_GROUPS)
-        unswitched = gy_sb[:].rearrange("b (j m r) -> b j m r", j=BLOCKS, m=M_GROUPS, r=R_COEFFS)
-        for j in range(BLOCKS):
-            if j < BLOCKS - 1:
-                nc.vector.tensor_copy(out=unswitched[:, j], in_=switched[:, j])
+
+        def unswitch(engine, half, pair):
+            source = g_sb[half][:].rearrange("b (r j m) -> b j m r", r=R_HALF, j=BLOCKS, m=M_GROUPS)
+            target = gy_sb[:].rearrange("b (j m h r) -> b h j m r", j=BLOCKS, m=M_GROUPS, h=2, r=R_HALF)
+            source = source[:, 2 * pair : 2 * pair + 2]
+            target = target[:, half, 2 * pair : 2 * pair + 2]
+            if engine == "vector":
+                nc.vector.tensor_copy(out=target, in_=source)
+            elif engine == "scalar":
+                nc.scalar.copy(out=target, in_=source)
             else:
-                nc.scalar.copy(out=unswitched[:, j], in_=switched[:, j])
+                nc.gpsimd.tensor_scalar(
+                    out=target, in0=source, scalar1=1.0, scalar2=0.0, op0=mybir.AluOpType.mult, op1=mybir.AluOpType.add
+                )
 
         gy_words = gy_sb[:].bitcast(F32)
         gy_grouped = keep.tile([P, BLOCKS * SAMPLES * 4], BF16, align_bytes=64)
@@ -78,46 +91,59 @@ def tile_switchnet_fstar_pa_s_kernel(tc, x, k1, b1, grad_out, out):
         gy_codes = keep.tile([P, BLOCKS * SAMPLES], U32, align_bytes=64)
         gy_scales = keep.tile([P, BLOCKS * SAMPLES], U8, align_bytes=64)
 
+        def copy(engine, target, source):
+            if engine == "vector":
+                nc.vector.tensor_copy(out=target, in_=source)
+            else:
+                nc.scalar.copy(out=target, in_=source)
+
+        banks = {}
+
         def flip_gradient(pair):
             bank = psum.tile([P, BANK], F32, tag="bank")
             for s in range(4):
                 col = pair * BANK + s * P
                 nc.tensor.transpose(bank[:, s * P : (s + 1) * P], gy_words[:, col : col + P], ident[:])
-            nc.vector.tensor_copy(
-                out=gy_grouped_words[:, pair * BANK : (pair + 1) * BANK].rearrange(
-                    "p (j b u) -> p j b u", j=2, b=SAMPLES, u=2
-                ),
-                in_=bank[:].rearrange("p (j u b) -> p j b u", j=2, u=2, b=SAMPLES),
+            banks["g%d" % pair] = bank
+
+        def group_gradient(engine, pair):
+            copy(
+                engine,
+                gy_grouped_words[:, pair * BANK : (pair + 1) * BANK].rearrange("p (j b u) -> p j b u", j=2, b=SAMPLES, u=2),
+                banks["g%d" % pair][:].rearrange("p (j u b) -> p j b u", j=2, u=2, b=SAMPLES),
             )
+
+        def quantise_gradient():
+            nc.vector.quantize_mx(out=gy_codes[:].bitcast(E5M2_X4), scales=gy_scales[:], in_=gy_grouped[:])
 
         k_codes = []
         k_scales = []
         for j in range(BLOCKS):
             k_codes.append(keep.tile([P, WINDOW], U32, name="k_codes%d" % j, align_bytes=64))
             k_scales.append(keep.tile([P, WINDOW], U8, name="k_scales%d" % j, align_bytes=64))
-
         k_grouped = []
-        for n, (j, first, rows) in enumerate(pieces):
-            k_grouped.append(keep.tile([P, rows * 4], BF16, name="k_grouped%d" % n, align_bytes=64))
+        for n in range(2 * BLOCKS):
+            k_grouped.append(keep.tile([P, ROWS * 4], BF16, name="k_grouped%d" % n, align_bytes=64))
 
         def flip_piece(n):
-            j, first, rows = pieces[n]
-            planes = 2 * rows // P
             words = k_sb[n][:].bitcast(F32)
             bank = psum.tile([P, BANK], F32, tag="bank")
-            for s in range(planes):
+            for s in range(4):
                 nc.tensor.transpose(bank[:, s * P : (s + 1) * P], words[:, s * P : (s + 1) * P], ident[:])
-            nc.scalar.copy(
-                out=k_grouped[n][:].bitcast(F32).rearrange("p (q s) -> p q s", s=planes),
-                in_=bank[:, : planes * P].rearrange("p (s q) -> p q s", s=planes),
+            banks["k%d" % n] = bank
+
+        def group_piece(engine, n):
+            copy(
+                engine,
+                k_grouped[n][:].bitcast(F32).rearrange("p (q s) -> p q s", s=4),
+                banks["k%d" % n][:].rearrange("p (s q) -> p q s", s=4),
             )
 
         def quantise_piece(n):
-            j, first, rows = pieces[n]
+            j, half = divmod(n, 2)
+            columns = slice(half * ROWS, (half + 1) * ROWS)
             nc.vector.quantize_mx(
-                out=k_codes[j][:, first : first + rows].bitcast(E4M3_X4),
-                scales=k_scales[j][:, first : first + rows],
-                in_=k_grouped[n][:],
+                out=k_codes[j][:, columns].bitcast(E4M3_X4), scales=k_scales[j][:, columns], in_=k_grouped[n][:]
             )
 
         out_sb = []
@@ -126,7 +152,6 @@ def tile_switchnet_fstar_pa_s_kernel(tc, x, k1, b1, grad_out, out):
         out_flat = out.rearrange("b g c -> b (g c)")
 
         def multiply_block(j):
-            block_row, block_col = divmod(j, 2)
             samples = slice(j * SAMPLES, (j + 1) * SAMPLES)
             acc = psum.tile([P, WINDOW], F32, tag="bank")
             nc.tensor.matmul_mx(
@@ -138,29 +163,67 @@ def tile_switchnet_fstar_pa_s_kernel(tc, x, k1, b1, grad_out, out):
                 start=True,
                 stop=True,
             )
-            on_grid = out_sb[block_row][:].rearrange("b (h w c x) -> b h c w x", h=2, c=2, x=BLOCK_ROW)
-            window = acc[:].rearrange("b (h w x) -> b h w x", h=2, x=BLOCK_ROW)
-            for half in range(2):
-                if block_col == 0:
-                    nc.scalar.copy(out=on_grid[:, half, block_col], in_=window[:, half])
-                else:
-                    nc.vector.tensor_copy(out=on_grid[:, half, block_col], in_=window[:, half])
-                if block_col == 1:
-                    first = (2 * block_row + half) * WINDOW
-                    nc.sync.dma_start(
-                        out=out_flat[:, first : first + WINDOW],
-                        in_=out_sb[block_row][:, half * WINDOW : (half + 1) * WINDOW],
-                    )
+            banks["o%d" % j] = acc
 
+        def leave(engine, j, half):
+            block_row, block_col = divmod(j, 2)
+            on_grid = out_sb[block_row][:].rearrange("b (h w c x) -> b h c w x", h=2, c=2, x=BLOCK_ROW)
+            window = banks["o%d" % j][:].rearrange("b (h w x) -> b h w x", h=2, x=BLOCK_ROW)
+            copy(engine, on_grid[:, half, block_col], window[:, half])
+
+        def store(block_row, half):
+            first = (2 * block_row + half) * WINDOW
+            nc.sync.dma_start(
+                out=out_flat[:, first : first + WINDOW],
+                in_=out_sb[block_row][:, half * WINDOW : (half + 1) * WINDOW],
+            )
+
+        unswitch("vector", 0, 1)
+        unswitch("scalar", 0, 0)
+        unswitch("vector", 1, 0)
+        unswitch("vector", 1, 1)
         flip_piece(0)
         flip_gradient(0)
         flip_piece(1)
         flip_gradient(1)
-        nc.vector.quantize_mx(out=gy_codes[:].bitcast(E5M2_X4), scales=gy_scales[:], in_=gy_grouped[:])
+        group_piece("scalar", 0)
+        group_gradient("vector", 0)
         quantise_piece(0)
+        group_piece("scalar", 1)
         quantise_piece(1)
-        for n in range(2, len(pieces)):
-            flip_piece(n)
-            quantise_piece(n)
-        for j in range(BLOCKS):
-            multiply_block(j)
+        flip_piece(2)
+        group_piece("vector", 2)
+        group_gradient("scalar", 1)
+        quantise_gradient()
+        flip_piece(3)
+        group_piece("scalar", 3)
+        quantise_piece(2)
+        quantise_piece(3)
+        flip_piece(4)
+        group_piece("scalar", 4)
+        quantise_piece(4)
+        flip_piece(5)
+        group_piece("scalar", 5)
+        quantise_piece(5)
+        flip_piece(6)
+        flip_piece(7)
+        group_piece("scalar", 6)
+        multiply_block(0)
+        multiply_block(1)
+        leave("vector", 0, 0)
+        group_piece("scalar", 7)
+        leave("scalar", 1, 0)
+        store(0, 0)
+        quantise_piece(6)
+        quantise_piece(7)
+        multiply_block(2)
+        multiply_block(3)
+        leave("vector", 1, 1)
+        leave("scalar", 0, 1)
+        store(0, 1)
+        leave("vector", 2, 0)
+        leave("scalar", 3, 0)
+        store(1, 0)
+        leave("vector", 2, 1)
+        leave("scalar", 3, 1)
+        store(1, 1)

@@ -21,7 +21,7 @@ R_HALF = R_COEFFS // 2
 BANK = 512
 BLOCK_ROW = 32
 ROWS = 256
-WARM_MATMULS = 4
+WARM_FIRST = 4
 
 FLOPS = 2 * SAMPLES * BLOCKS * WINDOW * FEATURES
 BYTES = 2 * BLOCKS * WINDOW * FEATURES + 2 * SAMPLES * BLOCKS * FEATURES + 4 * SAMPLES * BLOCKS * WINDOW
@@ -37,9 +37,12 @@ def tile_switchnet_fstar_pa_s_kernel(tc, x, k1, b1, grad_out, out):
         ident = keep.tile([P, P], F32)
         make_identity(nc, ident[:])
 
-        unread = psum.tile([P, BANK], F32, tag="bank")
-        for w in range(WARM_MATMULS):
-            nc.tensor.matmul(out=unread[:, :P], lhsT=ident[:], rhs=ident[:], start=True, stop=True)
+        def warm(count):
+            unread = psum.tile([P, BANK], F32, tag="bank")
+            for w in range(count):
+                nc.tensor.matmul(out=unread[:, :P], lhsT=ident[:], rhs=ident[:], start=True, stop=True)
+
+        warm(WARM_FIRST)
 
         g_flat = grad_out.rearrange("b a r -> b (a r)")
         half_columns = R_HALF * BLOCKS * M_GROUPS
@@ -186,6 +189,7 @@ def tile_switchnet_fstar_pa_s_kernel(tc, x, k1, b1, grad_out, out):
         flip_gradient(0)
         flip_piece(1)
         flip_gradient(1)
+        warm(1)
         group_piece("scalar", 0)
         group_gradient("vector", 0)
         quantise_piece(0)
@@ -202,6 +206,7 @@ def tile_switchnet_fstar_pa_s_kernel(tc, x, k1, b1, grad_out, out):
         flip_piece(4)
         group_piece("scalar", 4)
         quantise_piece(4)
+        warm(1)
         flip_piece(5)
         group_piece("scalar", 5)
         quantise_piece(5)

@@ -20,11 +20,22 @@ R_COEFFS = 64
 R_HALF = R_COEFFS // 2
 BANK = 512
 BLOCK_ROW = 32
-ROWS = 256
+HALF = WINDOW // 2
 WARM_FIRST = 4
 
 FLOPS = 2 * SAMPLES * BLOCKS * WINDOW * FEATURES
 BYTES = 2 * BLOCKS * WINDOW * FEATURES + 2 * SAMPLES * BLOCKS * FEATURES + 4 * SAMPLES * BLOCKS * WINDOW
+
+
+def pieces_of_k1():
+    pieces = []
+    for j in range(BLOCKS):
+        pieces.append((j, 0, HALF))
+        pieces.append((j, HALF, HALF))
+    j, first, rows = pieces.pop()
+    pieces.append((j, first, rows // 2))
+    pieces.append((j, first + rows // 2, rows // 2))
+    return pieces
 
 
 def tile_switchnet_fstar_pa_s_kernel(tc, x, k1, b1, grad_out, out):
@@ -48,17 +59,18 @@ def tile_switchnet_fstar_pa_s_kernel(tc, x, k1, b1, grad_out, out):
         half_columns = R_HALF * BLOCKS * M_GROUPS
         g_sb = {}
         k_sb = {}
+        pieces = pieces_of_k1()
 
         def load_gradient(half):
             g_sb[half] = keep.tile([P, half_columns], BF16, name="g_sb%d" % half)
             nc.sync.dma_start(out=g_sb[half][:], in_=g_flat[:, half * half_columns : (half + 1) * half_columns])
 
         def load_piece(n):
-            j, half = divmod(n, 2)
-            k_sb[n] = keep.tile([P, 2 * FEATURES], BF16, name="k_sb%d" % n)
+            j, first, rows = pieces[n]
+            k_sb[n] = keep.tile([P, rows // P * FEATURES], BF16, name="k_sb%d" % n)
             nc.sync.dma_start(
                 out=k_sb[n][:],
-                in_=k1[j, half * ROWS : (half + 1) * ROWS, :].rearrange("(q c) l -> q (c l)", c=2),
+                in_=k1[j, first : first + rows, :].rearrange("(q c) l -> q (c l)", c=rows // P),
             )
 
         load_gradient(0)
@@ -71,6 +83,7 @@ def tile_switchnet_fstar_pa_s_kernel(tc, x, k1, b1, grad_out, out):
         load_piece(5)
         load_piece(6)
         load_piece(7)
+        load_piece(8)
 
         gy_sb = keep.tile([P, BLOCKS * FEATURES], BF16)
 
@@ -125,26 +138,27 @@ def tile_switchnet_fstar_pa_s_kernel(tc, x, k1, b1, grad_out, out):
             k_codes.append(keep.tile([P, WINDOW], U32, name="k_codes%d" % j, align_bytes=64))
             k_scales.append(keep.tile([P, WINDOW], U8, name="k_scales%d" % j, align_bytes=64))
         k_grouped = []
-        for n in range(2 * BLOCKS):
-            k_grouped.append(keep.tile([P, ROWS * 4], BF16, name="k_grouped%d" % n, align_bytes=64))
+        for n, (j, first, rows) in enumerate(pieces):
+            k_grouped.append(keep.tile([P, rows * 4], BF16, name="k_grouped%d" % n, align_bytes=64))
 
         def flip_piece(n):
             words = k_sb[n][:].bitcast(F32)
             bank = psum.tile([P, BANK], F32, tag="bank")
-            for s in range(4):
+            for s in range(2 * pieces[n][2] // P):
                 nc.tensor.transpose(bank[:, s * P : (s + 1) * P], words[:, s * P : (s + 1) * P], ident[:])
             banks["k%d" % n] = bank
 
         def group_piece(engine, n):
+            planes = 2 * pieces[n][2] // P
             copy(
                 engine,
-                k_grouped[n][:].bitcast(F32).rearrange("p (q s) -> p q s", s=4),
-                banks["k%d" % n][:].rearrange("p (s q) -> p q s", s=4),
+                k_grouped[n][:].bitcast(F32).rearrange("p (q s) -> p q s", s=planes),
+                banks["k%d" % n][:, : planes * P].rearrange("p (s q) -> p q s", s=planes),
             )
 
         def quantise_piece(n):
-            j, half = divmod(n, 2)
-            columns = slice(half * ROWS, (half + 1) * ROWS)
+            j, first, rows = pieces[n]
+            columns = slice(first, first + rows)
             nc.vector.quantize_mx(
                 out=k_codes[j][:, columns].bitcast(E4M3_X4), scales=k_scales[j][:, columns], in_=k_grouped[n][:]
             )
@@ -189,13 +203,13 @@ def tile_switchnet_fstar_pa_s_kernel(tc, x, k1, b1, grad_out, out):
         flip_gradient(0)
         flip_piece(1)
         flip_gradient(1)
-        warm(1)
         group_piece("scalar", 0)
         group_gradient("vector", 0)
         quantise_piece(0)
         group_piece("scalar", 1)
         quantise_piece(1)
         flip_piece(2)
+        warm(1)
         group_piece("vector", 2)
         group_gradient("scalar", 1)
         quantise_gradient()
@@ -206,29 +220,32 @@ def tile_switchnet_fstar_pa_s_kernel(tc, x, k1, b1, grad_out, out):
         flip_piece(4)
         group_piece("scalar", 4)
         quantise_piece(4)
-        warm(1)
         flip_piece(5)
+        warm(1)
         group_piece("scalar", 5)
         quantise_piece(5)
         flip_piece(6)
         flip_piece(7)
+        flip_piece(8)
         group_piece("scalar", 6)
-        multiply_block(0)
-        multiply_block(1)
-        leave("vector", 0, 0)
         group_piece("scalar", 7)
-        leave("scalar", 1, 0)
-        store(0, 0)
+        group_piece("scalar", 8)
         quantise_piece(6)
         quantise_piece(7)
-        multiply_block(2)
-        multiply_block(3)
-        leave("vector", 1, 1)
+        quantise_piece(8)
+        multiply_block(0)
+        leave("scalar", 0, 0)
         leave("scalar", 0, 1)
+        multiply_block(1)
+        leave("vector", 1, 0)
+        store(0, 0)
+        leave("vector", 1, 1)
         store(0, 1)
-        leave("vector", 2, 0)
-        leave("scalar", 3, 0)
+        multiply_block(2)
+        leave("scalar", 2, 0)
+        leave("scalar", 2, 1)
+        multiply_block(3)
+        leave("vector", 3, 0)
         store(1, 0)
-        leave("vector", 2, 1)
-        leave("scalar", 3, 1)
+        leave("vector", 3, 1)
         store(1, 1)

from contextlib import ExitStack

import concourse.mybir as mybir
from concourse.masks import make_identity

BF16 = mybir.dt.bfloat16
F32 = mybir.dt.float32
U32 = mybir.dt.uint32
U8 = mybir.dt.uint8
E4M3_X4 = mybir.dt.float8_e4m3fn_x4
E5M2_X4 = mybir.dt.float8_e5m2_x4

P = 128
SAMPLES = 128
BLOCKS = 4
WINDOW = 512
FEATURES = 512
M_GROUPS = 8
R_COEFFS = 64
R_HALF = R_COEFFS // 2
BANK = 512
BLOCK_ROW = 32
HALF = WINDOW // 2
WARM_FIRST = 4

FLOPS = 2 * SAMPLES * BLOCKS * WINDOW * FEATURES
BYTES = 2 * BLOCKS * WINDOW * FEATURES + 2 * SAMPLES * BLOCKS * FEATURES + 4 * SAMPLES * BLOCKS * WINDOW


def pieces_of_k1():
    pieces = []
    for j in range(BLOCKS):
        pieces.append((j, 0, HALF))
        pieces.append((j, HALF, HALF))
    j, first, rows = pieces.pop()
    pieces.append((j, first, rows // 2))
    pieces.append((j, first + rows // 2, rows // 2))
    return pieces


def tile_switchnet_fstar_pa_s_kernel(tc, x, k1, b1, grad_out, out):
    nc = tc.nc
    with ExitStack() as stack:
        keep = stack.enter_context(tc.tile_pool(name="keep", bufs=1))
        psum = stack.enter_context(tc.psum_pool(name="psum", bufs=8))
        stack.enter_context(tc.manual_schedule())

        ident = keep.tile([P, P], F32)
        make_identity(nc, ident[:])

        def warm(count):
            unread = psum.tile([P, BANK], F32, tag="bank")
            for w in range(count):
                nc.tensor.matmul(out=unread[:, :P], lhsT=ident[:], rhs=ident[:], start=True, stop=True)

        warm(WARM_FIRST)

        g_flat = grad_out.rearrange("b a r -> b (a r)")
        half_columns = R_HALF * BLOCKS * M_GROUPS
        g_sb = {}
        k_sb = {}
        pieces = pieces_of_k1()

        def load_gradient(half):
            g_sb[half] = keep.tile([P, half_columns], BF16, name="g_sb%d" % half)
            nc.sync.dma_start(out=g_sb[half][:], in_=g_flat[:, half * half_columns : (half + 1) * half_columns])

        def load_piece(n):
            j, first, rows = pieces[n]
            k_sb[n] = keep.tile([P, rows // P * FEATURES], BF16, name="k_sb%d" % n)
            nc.sync.dma_start(
                out=k_sb[n][:],
                in_=k1[j, first : first + rows, :].rearrange("(q c) l -> q (c l)", c=rows // P),
            )

        load_gradient(0)
        load_gradient(1)
        load_piece(0)
        load_piece(1)
        load_piece(2)
        load_piece(3)
        load_piece(4)
        load_piece(5)
        load_piece(6)
        load_piece(7)
        load_piece(8)

        gy_sb = keep.tile([P, BLOCKS * FEATURES], BF16)

        def unswitch(engine, half, pair):
            source = g_sb[half][:].rearrange("b (r j m) -> b j m r", r=R_HALF, j=BLOCKS, m=M_GROUPS)
            target = gy_sb[:].rearrange("b (j m h r) -> b h j m r", j=BLOCKS, m=M_GROUPS, h=2, r=R_HALF)
            source = source[:, 2 * pair : 2 * pair + 2]
            target = target[:, half, 2 * pair : 2 * pair + 2]
            if engine == "vector":
                nc.vector.tensor_copy(out=target, in_=source)
            elif engine == "scalar":
                nc.scalar.copy(out=target, in_=source)
            else:
                nc.gpsimd.tensor_scalar(
                    out=target, in0=source, scalar1=1.0, scalar2=0.0, op0=mybir.AluOpType.mult, op1=mybir.AluOpType.add
                )

        gy_words = gy_sb[:].bitcast(F32)
        gy_grouped = keep.tile([P, BLOCKS * SAMPLES * 4], BF16, align_bytes=64)
        gy_grouped_words = gy_grouped[:].bitcast(F32)
        gy_codes = keep.tile([P, BLOCKS * SAMPLES], U32, align_bytes=64)
        gy_scales = keep.tile([P, BLOCKS * SAMPLES], U8, align_bytes=64)

        def copy(engine, target, source):
            if engine == "vector":
                nc.vector.tensor_copy(out=target, in_=source)
            else:
                nc.scalar.copy(out=target, in_=source)

        banks = {}

        def flip_gradient(pair):
            bank = psum.tile([P, BANK], F32, tag="bank")
            for s in range(4):
                col = pair * BANK + s * P
                nc.tensor.transpose(bank[:, s * P : (s + 1) * P], gy_words[:, col : col + P], ident[:])
            banks["g%d" % pair] = bank

        def group_gradient(engine, pair):
            copy(
                engine,
                gy_grouped_words[:, pair * BANK : (pair + 1) * BANK].rearrange("p (j b u) -> p j b u", j=2, b=SAMPLES, u=2),
                banks["g%d" % pair][:].rearrange("p (j u b) -> p j b u", j=2, u=2, b=SAMPLES),
            )

        def quantise_gradient():
            nc.vector.quantize_mx(out=gy_codes[:].bitcast(E5M2_X4), scales=gy_scales[:], in_=gy_grouped[:])

        k_codes = []
        k_scales = []
        for j in range(BLOCKS):
            k_codes.append(keep.tile([P, WINDOW], U32, name="k_codes%d" % j, align_bytes=64))
            k_scales.append(keep.tile([P, WINDOW], U8, name="k_scales%d" % j, align_bytes=64))
        k_grouped = []
        for n, (j, first, rows) in enumerate(pieces):
            k_grouped.append(keep.tile([P, rows * 4], BF16, name="k_grouped%d" % n, align_bytes=64))

        def flip_piece(n):
            words = k_sb[n][:].bitcast(F32)
            bank = psum.tile([P, BANK], F32, tag="bank")
            for s in range(2 * pieces[n][2] // P):
                nc.tensor.transpose(bank[:, s * P : (s + 1) * P], words[:, s * P : (s + 1) * P], ident[:])
            banks["k%d" % n] = bank

        def group_piece(engine, n):
            planes = 2 * pieces[n][2] // P
            copy(
                engine,
                k_grouped[n][:].bitcast(F32).rearrange("p (q s) -> p q s", s=planes),
                banks["k%d" % n][:, : planes * P].rearrange("p (s q) -> p q s", s=planes),
            )

        def quantise_piece(n):
            j, first, rows = pieces[n]
            columns = slice(first, first + rows)
            nc.vector.quantize_mx(
                out=k_codes[j][:, columns].bitcast(E4M3_X4), scales=k_scales[j][:, columns], in_=k_grouped[n][:]
            )

        out_sb = []
        for block_row in range(2):
            out_sb.append(keep.tile([P, 2 * WINDOW], F32, name="out_sb%d" % block_row))
        out_flat = out.rearrange("b g c -> b (g c)")

        def multiply_block(j):
            samples = slice(j * SAMPLES, (j + 1) * SAMPLES)
            acc = psum.tile([P, WINDOW], F32, tag="bank")
            nc.tensor.matmul_mx(
                out=acc[:],
                lhsT=gy_codes[:, samples].bitcast(E5M2_X4),
                lhsT_scale=gy_scales[:, samples],
                rhs=k_codes[j][:].bitcast(E4M3_X4),
                rhs_scale=k_scales[j][:],
                start=True,
                stop=True,
            )
            banks["o%d" % j] = acc

        def leave(engine, j, half):
            block_row, block_col = divmod(j, 2)
            on_grid = out_sb[block_row][:].rearrange("b (h w c x) -> b h c w x", h=2, c=2, x=BLOCK_ROW)
            window = banks["o%d" % j][:].rearrange("b (h w x) -> b h w x", h=2, x=BLOCK_ROW)
            copy(engine, on_grid[:, half, block_col], window[:, half])

        def store(block_row, half):
            first = (2 * block_row + half) * WINDOW
            nc.sync.dma_start(
                out=out_flat[:, first : first + WINDOW],
                in_=out_sb[block_row][:, half * WINDOW : (half + 1) * WINDOW],
            )

        unswitch("vector", 0, 1)
        unswitch("scalar", 0, 0)
        unswitch("vector", 1, 0)
        unswitch("vector", 1, 1)
        flip_piece(0)
        flip_gradient(0)
        flip_piece(1)
        flip_gradient(1)
        group_piece("scalar", 0)
        group_gradient("vector", 0)
        quantise_piece(0)
        group_piece("scalar", 1)
        quantise_piece(1)
        flip_piece(2)
        warm(1)
        group_piece("vector", 2)
        group_gradient("scalar", 1)
        quantise_gradient()
        flip_piece(3)
        group_piece("scalar", 3)
        quantise_piece(2)
        quantise_piece(3)
        flip_piece(4)
        group_piece("scalar", 4)
        quantise_piece(4)
        flip_piece(5)
        warm(1)
        group_piece("scalar", 5)
        quantise_piece(5)
        flip_piece(6)
        flip_piece(7)
        flip_piece(8)
        group_piece("scalar", 6)
        group_piece("scalar", 7)
        group_piece("scalar", 8)
        quantise_piece(6)
        quantise_piece(7)
        quantise_piece(8)
        multiply_block(0)
        leave("scalar", 0, 0)
        leave("scalar", 0, 1)
        multiply_block(1)
        leave("vector", 1, 0)
        store(0, 0)
        leave("vector", 1, 1)
        store(0, 1)
        multiply_block(2)
        leave("scalar", 2, 0)
        leave("scalar", 2, 1)
        multiply_block(3)
        leave("vector", 3, 0)
        store(1, 0)
        leave("vector", 3, 1)
        store(1, 1)
